import numpy as np
import ml_dtypes


def mxq(x, axis, fmt="e4m3"):
    dtype, down = {"e4m3": (ml_dtypes.float8_e4m3fn, 7), "e5m2": (ml_dtypes.float8_e5m2, 14)}[fmt]
    v = np.moveaxis(np.asarray(x, np.float32).astype(ml_dtypes.bfloat16).astype(np.float64), axis, -1)
    blocks = v.reshape(v.shape[:-1] + (-1, 32))
    amax = np.abs(blocks).max(-1, keepdims=True)
    byte = np.maximum(np.where(amax > 0, np.frexp(amax)[1] - 1 + 127, 0) - down, 1)
    scale = np.exp2(byte - 127.0)
    codes = (blocks / scale).astype(np.float32).astype(dtype).astype(np.float64)
    return np.moveaxis((codes * scale).reshape(v.shape), -1, axis)


WIDE = False


def mx_kscale(k):
    if not WIDE:
        return np.ones(k)
    levels = np.array([10, -10, 5, -5, 0])
    a = np.random.permutation(np.resize(levels, k // 512 * 4)).reshape(k // 512, 4)
    idx = np.arange(k)
    return np.exp2(a[idx // 512, idx % 128 // 32])


BF16 = ml_dtypes.bfloat16


def bf(x):
    return np.asarray(x, np.float32).astype(BF16)


def f64(x):
    return np.asarray(x).astype(np.float64)


E2M1 = np.array([0.0, 0.5, 1.0, 1.5, 2.0, 3.0, 4.0, 6.0, -0.0, -0.5, -1.0, -1.5, -2.0, -3.0, -4.0, -6.0])


def pack_weight(w, fmt):
    k, n = w.shape
    w = f64(bf(w)).reshape(k // 32, 32, n)
    amax = np.abs(w).max(1)
    if fmt == "e4m3":
        byte = np.frexp(amax)[1] - 1 + 127 - 7
    else:
        mant, ex = np.frexp(amax / 6.0)
        byte = np.where(mant > 0.5, ex, ex - 1) + 127
    byte = np.clip(np.where(amax > 0, byte, 1), 1, 254)
    scaled = (w * np.exp2(127.0 - byte)[:, None, :]).reshape(k, n).astype(np.float32)
    by_word = np.ascontiguousarray(scaled.reshape(k // 512, 128, 4, n).transpose(0, 1, 3, 2))
    if fmt == "e4m3":
        words = by_word.astype(ml_dtypes.float8_e4m3fn).view(np.uint8)
    else:
        c = by_word.astype(ml_dtypes.float4_e2m1fn).view(np.uint8) & 0xF
        words = c[..., 0::2] | (c[..., 1::2] << 4)
    return np.ascontiguousarray(words), np.ascontiguousarray(byte.astype(np.uint8).reshape(k // 512, 16, n))


def unpack_weight(words, scales, fmt):
    g, p, n, _ = words.shape
    if fmt == "e4m3":
        vals = np.ascontiguousarray(words).view(ml_dtypes.float8_e4m3fn).astype(np.float64)
    else:
        nib = np.empty((g, p, n, 4), np.uint8)
        nib[..., 0::2] = words & 0xF
        nib[..., 1::2] = words >> 4
        vals = E2M1[nib]
    vals = vals * np.repeat(np.exp2(scales.astype(np.float64) - 127.0), 8, axis=1)[..., None]
    return vals.transpose(0, 1, 3, 2).reshape(g * 512, n)


S, E, HQ, HK, D, C = 8192, 1024, 4, 4, 32, 512


def rotate_half(t):
    t1, t2 = np.split(t, 2, axis=-1)
    return np.concatenate([-t2, t1], axis=-1)


def setup_inputs():
    s = mx_kscale(E)
    theta = np.random.uniform(0.0, 2.0 * np.pi, (S, D // 2))
    theta = np.concatenate([theta, theta], axis=-1)
    x = bf(np.random.standard_normal((S, E)) * s)
    w_q = np.random.standard_normal((HQ * D, E)) * 1.4 / np.sqrt(E) / s[None, :]
    w_k = np.random.standard_normal((HK * D, E)) * 1.4 / np.sqrt(E) / s[None, :]
    w_v = np.random.standard_normal((HK * D, E)) / np.sqrt(E) / s[None, :]
    w_q_words, w_q_scales = pack_weight(w_q.T, "e4m3")
    w_k_words, w_k_scales = pack_weight(w_k.T, "e4m3")
    w_v_words, w_v_scales = pack_weight(w_v.T, "e4m3")
    return {"x": x,
            "w_q_words": w_q_words, "w_q_scales": w_q_scales,
            "w_k_words": w_k_words, "w_k_scales": w_k_scales,
            "w_v_words": w_v_words, "w_v_scales": w_v_scales,
            "cos_tab": bf(np.cos(theta)), "sin_tab": bf(np.sin(theta))}


def reference(x, w_q_words, w_q_scales, w_k_words, w_k_scales, w_v_words, w_v_scales, cos_tab, sin_tab):
    xq = mxq(f64(x), 1, "e4m3")
    q = (xq @ unpack_weight(w_q_words, w_q_scales, "e4m3")).reshape(S, HQ, D)
    k = (xq @ unpack_weight(w_k_words, w_k_scales, "e4m3")).reshape(S, HK, D)
    v = (xq @ unpack_weight(w_v_words, w_v_scales, "e4m3")).reshape(S, HK, D)
    c = f64(cos_tab).reshape(S, 1, D)
    sn = f64(sin_tab).reshape(S, 1, D)
    q_rot = q * c + rotate_half(q) * sn
    k_rot = k * c + rotate_half(k) * sn
    return q_rot, k_rot, v

@@ -1,0 +1,223 @@
+from contextlib import ExitStack
+
+import concourse.mybir as mybir
+from concourse.masks import make_identity
+
+BF16 = mybir.dt.bfloat16
+F32 = mybir.dt.float32
+I32 = mybir.dt.int32
+U32 = mybir.dt.uint32
+U8 = mybir.dt.uint8
+FP8X4 = mybir.dt.float8_e4m3fn_x4
+ALU = mybir.AluOpType
+
+P = 128
+ROWS = 8192
+K = 1024
+K_PASS = 4 * P
+PASSES = K // K_PASS
+WORDS_PASS = K_PASS // 2
+HEADS = 4
+HEAD_DIM = 32
+HALF = HEAD_DIM // 2
+FEATURES = HEADS * HEAD_DIM
+ROW_TILES = ROWS // P
+PAIR = 2
+RUN_PAIRS = 2
+RUN_TILES = RUN_PAIRS * PAIR
+RUNS = ROW_TILES // RUN_TILES
+LOADS_AHEAD = 6
+STORE_TILES = 8
+
+FLOPS = 2 * ROWS * K * 3 * FEATURES
+
+
+def tile_groupedqueryattention_pa_t_kernel(
+    tc,
+    x,
+    w_q_words,
+    w_q_scales,
+    w_k_words,
+    w_k_scales,
+    w_v_words,
+    w_v_scales,
+    cos_tab,
+    sin_tab,
+    out_0,
+    out_1,
+    out_2,
+):
+    nc = tc.nc
+
+    x_rows = x.rearrange("(p t) k -> p t k", t=ROW_TILES)
+    cos_rows = cos_tab.rearrange("(p t) d -> p t d", t=ROW_TILES)
+    sin_rows = sin_tab.rearrange("(p t) d -> p t d", t=ROW_TILES)
+    q_rows = out_0.rearrange("(p t) h d -> p t (h d)", t=ROW_TILES)
+    k_rows = out_1.rearrange("(p t) h d -> p t (h d)", t=ROW_TILES)
+    v_rows = out_2.rearrange("(p t) h d -> p t (h d)", t=ROW_TILES)
+
+    with ExitStack() as ctx:
+        const = ctx.enter_context(tc.tile_pool(name="const", bufs=1))
+        x_pool = ctx.enter_context(tc.tile_pool(name="x", bufs=LOADS_AHEAD + 1))
+        grouped_pool = ctx.enter_context(tc.tile_pool(name="grouped", bufs=2 * RUN_PAIRS))
+        codes_pool = ctx.enter_context(tc.tile_pool(name="codes", bufs=2 * RUN_PAIRS))
+        cross_pool = ctx.enter_context(tc.tile_pool(name="cross", bufs=2 * RUN_PAIRS))
+        result_pool = ctx.enter_context(tc.tile_pool(name="result", bufs=4))
+        xt_pool = ctx.enter_context(tc.psum_pool(name="xt", bufs=RUN_TILES))
+        qk_pool = ctx.enter_context(tc.psum_pool(name="qk", bufs=RUN_PAIRS))
+        v_pool = ctx.enter_context(tc.psum_pool(name="v", bufs=RUN_PAIRS))
+        ctx.enter_context(tc.manual_schedule())
+
+        identity = const.tile([P, P], F32, name="identity")
+        make_identity(nc, identity[:])
+
+        w_codes = const.tile([P, PASSES, 3 * FEATURES], U32, name="w_codes", align_bytes=64)
+        w_scales = const.tile([P, PASSES, 3 * FEATURES], U8, name="w_scales", align_bytes=64)
+        nc.vector.memset(w_scales[:].rearrange("p g n -> p (g n)").bitcast(I32), 0)
+
+        x_sb = {}
+
+        def load_x(run):
+            first = run * RUN_TILES
+            x_sb[run] = x_pool.tile([P, RUN_TILES, K], BF16, name="x_sb")
+            nc.sync.dma_start(out=x_sb[run][:], in_=x_rows[:, first : first + RUN_TILES, :])
+
+        load_x(0)
+        for w, (words, scales) in enumerate(
+            ((w_q_words, w_q_scales), (w_k_words, w_k_scales), (w_v_words, w_v_scales))
+        ):
+            cols = slice(w * FEATURES, (w + 1) * FEATURES)
+            nc.gpsimd.dma_start(
+                out=w_codes[:, :, cols].bitcast(F32),
+                in_=words.rearrange("g p n t -> p g (n t)").bitcast(F32),
+            )
+            for quadrant in range(4):
+                nc.sync.dma_start(
+                    out=w_scales[32 * quadrant : 32 * quadrant + 4, :, cols].bitcast(I32),
+                    in_=scales[:, 4 * quadrant : 4 * quadrant + 4, :].rearrange("g r n -> r g n").bitcast(I32),
+                )
+        load_x(1)
+        cos_sb = const.tile([P, ROW_TILES, HEAD_DIM], BF16, name="cos_sb")
+        sin_sb = const.tile([P, ROW_TILES, HEAD_DIM], BF16, name="sin_sb")
+        nc.sync.dma_start(out=cos_sb[:], in_=cos_rows)
+        nc.sync.dma_start(out=sin_sb[:], in_=sin_rows)
+        for run in range(2, LOADS_AHEAD):
+            load_x(run)
+
+        x_codes = {}
+        x_scales = {}
+
+        def transpose_and_quantise(pair):
+            grouped = grouped_pool.tile([P, PAIR, PASSES, P, 4], BF16, name="grouped", align_bytes=64)
+            for i in range(PAIR):
+                row_tile = pair * PAIR + i
+                words = x_sb[row_tile // RUN_TILES][:, row_tile % RUN_TILES, :].bitcast(F32)
+                xt = xt_pool.tile([P, PASSES, 2, P], F32, name="xt")
+                for g in range(PASSES):
+                    for u in range(2):
+                        nc.tensor.transpose(
+                            xt[:, g, u, :],
+                            words[:, g * WORDS_PASS + u : (g + 1) * WORDS_PASS : 2],
+                            identity[:],
+                        )
+                nc.scalar.copy(
+                    out=grouped[:, i, :, :, :]
+                    .rearrange("p g r j -> p (g r j)")
+                    .bitcast(F32)
+                    .rearrange("p (g r u) -> p g r u", g=PASSES, u=2),
+                    in_=xt[:].rearrange("p g u r -> p g r u"),
+                )
+            x_codes[pair] = codes_pool.tile([P, PAIR, PASSES, P], U32, name="x_codes", align_bytes=64)
+            x_scales[pair] = codes_pool.tile([P, PAIR, PASSES, P], U8, name="x_scales", align_bytes=64)
+            nc.vector.quantize_mx(
+                out=x_codes[pair][:].rearrange("p i g r -> p (i g r)").bitcast(FP8X4),
+                scales=x_scales[pair][:].rearrange("p i g r -> p (i g r)"),
+                in_=grouped[:].rearrange("p i g r j -> p (i g r j)"),
+            )
+
+        results = {}
+
+        def project(out, pair, i, cols):
+            for g in range(PASSES):
+                nc.tensor.matmul_mx(
+                    out=out,
+                    lhsT=x_codes[pair][:, i, g, :].bitcast(FP8X4),
+                    lhsT_scale=x_scales[pair][:, i, g, :],
+                    rhs=w_codes[:, g, cols].bitcast(FP8X4),
+                    rhs_scale=w_scales[:, g, cols],
+                    start=(g == 0),
+                    stop=(g == PASSES - 1),
+                )
+
+        def multiply_and_rotate(pair):
+            first = pair * PAIR
+            place = first % STORE_TILES
+            if place == 0:
+                results["qk"] = result_pool.tile([P, 2, STORE_TILES, FEATURES], F32, name="qk_sb")
+                results["v"] = result_pool.tile([P, STORE_TILES, FEATURES], F32, name="v_sb")
+            qk_sb = results["qk"]
+            v_sb = results["v"]
+
+            qk_ps = qk_pool.tile([P, PAIR, 2 * FEATURES], F32, name="qk_ps")
+            v_ps = v_pool.tile([P, PAIR, FEATURES], F32, name="v_ps")
+            for i in range(PAIR):
+                project(qk_ps[:, i, :], pair, i, slice(0, 2 * FEATURES))
+                project(v_ps[:, i, :], pair, i, slice(2 * FEATURES, 3 * FEATURES))
+
+            nc.scalar.copy(out=v_sb[:, place : place + PAIR, :], in_=v_ps[:])
+
+            table_shape = [P, PAIR, 2 * HEADS, HEAD_DIM]
+            tiles = slice(first, first + PAIR)
+            cross = cross_pool.tile([P, 2, PAIR, FEATURES], F32, name="cross")
+            nc.vector.tensor_tensor(
+                out=qk_sb[:, :, place : place + PAIR, :].rearrange("p w i f -> p i w f"),
+                in0=qk_ps[:],
+                in1=cos_sb[:, tiles, :].unsqueeze(2).to_broadcast(table_shape),
+                op=ALU.mult,
+            )
+            nc.vector.tensor_tensor(
+                out=cross[:].rearrange("p w i f -> p i w f"),
+                in0=qk_ps[:],
+                in1=sin_swapped[:, tiles, :].unsqueeze(2).to_broadcast(table_shape),
+                op=ALU.mult,
+            )
+            halves = "p w i (h f j) -> p w (i h) f j"
+            straight_halves = qk_sb[:, :, place : place + PAIR, :].rearrange(halves, f=2, j=HALF)
+            cross_halves = cross[:].rearrange(halves, f=2, j=HALF)
+            nc.gpsimd.tensor_tensor(
+                out=straight_halves[:, :, :, 0, :],
+                in0=straight_halves[:, :, :, 0, :],
+                in1=cross_halves[:, :, :, 1, :],
+                op=ALU.subtract,
+            )
+            nc.gpsimd.tensor_tensor(
+                out=straight_halves[:, :, :, 1, :],
+                in0=straight_halves[:, :, :, 1, :],
+                in1=cross_halves[:, :, :, 0, :],
+                op=ALU.add,
+            )
+
+            if place + PAIR == STORE_TILES:
+                stored = slice(first + PAIR - STORE_TILES, first + PAIR)
+                nc.sync.dma_start(out=v_rows[:, stored, :], in_=v_sb[:])
+                nc.sync.dma_start(out=q_rows[:, stored, :], in_=qk_sb[:, 0, :, :])
+                nc.sync.dma_start(out=k_rows[:, stored, :], in_=qk_sb[:, 1, :, :])
+
+        def pairs_of(run):
+            return range(run * RUN_PAIRS, (run + 1) * RUN_PAIRS)
+
+        for pair in pairs_of(0):
+            transpose_and_quantise(pair)
+
+        sin_swapped = const.tile([P, ROW_TILES, HEAD_DIM], BF16, name="sin_swapped")
+        nc.vector.tensor_copy(out=sin_swapped[:, :, 0:HALF], in_=sin_sb[:, :, HALF:HEAD_DIM])
+        nc.vector.tensor_copy(out=sin_swapped[:, :, HALF:HEAD_DIM], in_=sin_sb[:, :, 0:HALF])
+
+        for run in range(RUNS):
+            if run + 1 < RUNS:
+                for pair in pairs_of(run + 1):
+                    transpose_and_quantise(pair)
+            if run + LOADS_AHEAD < RUNS:
+                load_x(run + LOADS_AHEAD)
+            for pair in pairs_of(run):
+                multiply_and_rotate(pair)

@@ -26,8 +26,11 @@ PAIR = 2
 RUN_PAIRS = 2
 RUN_TILES = RUN_PAIRS * PAIR
 RUNS = ROW_TILES // RUN_TILES
+LEAD = 2
 LOADS_AHEAD = 6
 STORE_TILES = 8
+FIRST_TABLE_TILES = 8
+TAIL_RUNS = 2
 
 FLOPS = 2 * ROWS * K * 3 * FEATURES
 
@@ -59,13 +62,13 @@ def tile_groupedqueryattention_pa_t_kernel(
     with ExitStack() as ctx:
         const = ctx.enter_context(tc.tile_pool(name="const", bufs=1))
         x_pool = ctx.enter_context(tc.tile_pool(name="x", bufs=LOADS_AHEAD + 1))
-        grouped_pool = ctx.enter_context(tc.tile_pool(name="grouped", bufs=2 * RUN_PAIRS))
-        codes_pool = ctx.enter_context(tc.tile_pool(name="codes", bufs=2 * RUN_PAIRS))
-        cross_pool = ctx.enter_context(tc.tile_pool(name="cross", bufs=2 * RUN_PAIRS))
-        result_pool = ctx.enter_context(tc.tile_pool(name="result", bufs=4))
+        grouped_pool = ctx.enter_context(tc.tile_pool(name="grouped", bufs=3))
+        codes_pool = ctx.enter_context(tc.tile_pool(name="codes", bufs=LEAD + 2))
+        prod_pool = ctx.enter_context(tc.tile_pool(name="prod", bufs=3))
+        result_pool = ctx.enter_context(tc.tile_pool(name="result", bufs=3))
         xt_pool = ctx.enter_context(tc.psum_pool(name="xt", bufs=RUN_TILES))
         qk_pool = ctx.enter_context(tc.psum_pool(name="qk", bufs=RUN_PAIRS))
-        v_pool = ctx.enter_context(tc.psum_pool(name="v", bufs=RUN_PAIRS))
+        v_pool = ctx.enter_context(tc.psum_pool(name="v", bufs=2))
         ctx.enter_context(tc.manual_schedule())
 
         identity = const.tile([P, P], F32, name="identity")
@@ -77,41 +80,67 @@ def tile_groupedqueryattention_pa_t_kernel(
 
         x_sb = {}
 
-        def load_x(run):
-            first = run * RUN_TILES
+        def load_x(queue, run, pieces):
             x_sb[run] = x_pool.tile([P, RUN_TILES, K], BF16, name="x_sb")
-            nc.sync.dma_start(out=x_sb[run][:], in_=x_rows[:, first : first + RUN_TILES, :])
+            at = 0
+            for tiles in pieces:
+                first = run * RUN_TILES + at
+                queue.dma_start(out=x_sb[run][:, at : at + tiles, :], in_=x_rows[:, first : first + tiles, :])
+                at += tiles
 
-        load_x(0)
-        for w, (words, scales) in enumerate(
-            ((w_q_words, w_q_scales), (w_k_words, w_k_scales), (w_v_words, w_v_scales))
-        ):
-            cols = slice(w * FEATURES, (w + 1) * FEATURES)
-            nc.gpsimd.dma_start(
-                out=w_codes[:, :, cols].bitcast(F32),
-                in_=words.rearrange("g p n t -> p g (n t)").bitcast(F32),
-            )
-            for quadrant in range(4):
+        weights = ((w_q_words, w_q_scales), (w_k_words, w_k_scales), (w_v_words, w_v_scales))
+        cos_sb = const.tile([P, ROW_TILES, HEAD_DIM], BF16, name="cos_sb")
+        sin_sb = const.tile([P, ROW_TILES, HEAD_DIM], BF16, name="sin_sb")
+
+        def load_tables(tiles):
+            nc.sync.dma_start(out=cos_sb[:, tiles, :], in_=cos_rows[:, tiles, :])
+            nc.sync.dma_start(out=sin_sb[:, tiles, :], in_=sin_rows[:, tiles, :])
+
+        def load_scales(which):
+            for n in which:
+                scales = weights[n // 4][1]
+                quadrant = n % 4
+                cols = slice((n // 4) * FEATURES, (n // 4 + 1) * FEATURES)
                 nc.sync.dma_start(
                     out=w_scales[32 * quadrant : 32 * quadrant + 4, :, cols].bitcast(I32),
                     in_=scales[:, 4 * quadrant : 4 * quadrant + 4, :].rearrange("g r n -> r g n").bitcast(I32),
                 )
-        load_x(1)
-        cos_sb = const.tile([P, ROW_TILES, HEAD_DIM], BF16, name="cos_sb")
-        sin_sb = const.tile([P, ROW_TILES, HEAD_DIM], BF16, name="sin_sb")
-        nc.sync.dma_start(out=cos_sb[:], in_=cos_rows)
-        nc.sync.dma_start(out=sin_sb[:], in_=sin_rows)
-        for run in range(2, LOADS_AHEAD):
-            load_x(run)
 
+        load_x(nc.scalar, 0, (1, 1, 2))
+        load_scales(range(0, 5))
+        load_x(nc.sync, 1, (4,))
+        load_scales(range(5, 9))
+        load_x(nc.sync, 2, (4,))
+        load_scales(range(9, 12))
+        for w, (words, scales) in enumerate(weights):
+            cols = slice(w * FEATURES, (w + 1) * FEATURES)
+            nc.sync.dma_start(
+                out=w_codes[:, :, cols].bitcast(I32),
+                in_=words.rearrange("g p n t -> p g (n t)").bitcast(I32),
+            )
+        load_tables(slice(0, FIRST_TABLE_TILES))
+        load_x(nc.sync, 3, (4,))
+        load_x(nc.sync, 4, (4,))
+        load_tables(slice(FIRST_TABLE_TILES, ROW_TILES))
+        load_x(nc.sync, 5, (4,))
+
+        table_lo = const.tile([P, ROW_TILES, HEAD_DIM], BF16, name="table_lo")
+        table_hi = const.tile([P, ROW_TILES, HEAD_DIM], BF16, name="table_hi")
+
+        def make_tables(tiles):
+            nc.vector.tensor_copy(out=table_lo[:, tiles, 0:HALF], in_=cos_sb[:, tiles, 0:HALF])
+            nc.vector.tensor_scalar_mul(out=table_lo[:, tiles, HALF:HEAD_DIM], in0=sin_sb[:, tiles, 0:HALF], scalar1=-1.0)
+            nc.vector.tensor_copy(out=table_hi[:, tiles, 0:HALF], in_=sin_sb[:, tiles, HALF:HEAD_DIM])
+            nc.vector.tensor_copy(out=table_hi[:, tiles, HALF:HEAD_DIM], in_=cos_sb[:, tiles, HALF:HEAD_DIM])
+
+        grouped = {}
         x_codes = {}
         x_scales = {}
 
-        def transpose_and_quantise(pair):
-            grouped = grouped_pool.tile([P, PAIR, PASSES, P, 4], BF16, name="grouped", align_bytes=64)
-            for i in range(PAIR):
-                row_tile = pair * PAIR + i
-                words = x_sb[row_tile // RUN_TILES][:, row_tile % RUN_TILES, :].bitcast(F32)
+        def transpose(run):
+            grouped[run] = grouped_pool.tile([P, RUN_TILES, PASSES, P, 4], BF16, name="grouped", align_bytes=64)
+            for i in range(RUN_TILES):
+                words = x_sb[run][:, i, :].bitcast(F32)
                 xt = xt_pool.tile([P, PASSES, 2, P], F32, name="xt")
                 for g in range(PASSES):
                     for u in range(2):
@@ -121,103 +150,121 @@ def tile_groupedqueryattention_pa_t_kernel(
                             identity[:],
                         )
                 nc.scalar.copy(
-                    out=grouped[:, i, :, :, :]
+                    out=grouped[run][:, i, :, :, :]
                     .rearrange("p g r j -> p (g r j)")
                     .bitcast(F32)
                     .rearrange("p (g r u) -> p g r u", g=PASSES, u=2),
                     in_=xt[:].rearrange("p g u r -> p g r u"),
                 )
-            x_codes[pair] = codes_pool.tile([P, PAIR, PASSES, P], U32, name="x_codes", align_bytes=64)
-            x_scales[pair] = codes_pool.tile([P, PAIR, PASSES, P], U8, name="x_scales", align_bytes=64)
+
+        def quantise(run):
+            x_codes[run] = codes_pool.tile([P, RUN_TILES, PASSES, P], U32, name="x_codes", align_bytes=64)
+            x_scales[run] = codes_pool.tile([P, RUN_TILES, PASSES, P], U8, name="x_scales", align_bytes=64)
             nc.vector.quantize_mx(
-                out=x_codes[pair][:].rearrange("p i g r -> p (i g r)").bitcast(FP8X4),
-                scales=x_scales[pair][:].rearrange("p i g r -> p (i g r)"),
-                in_=grouped[:].rearrange("p i g r j -> p (i g r j)"),
+                out=x_codes[run][:].rearrange("p i g r -> p (i g r)").bitcast(FP8X4),
+                scales=x_scales[run][:].rearrange("p i g r -> p (i g r)"),
+                in_=grouped[run][:].rearrange("p i g r j -> p (i g r j)"),
             )
 
-        results = {}
-
-        def project(out, pair, i, cols):
+        def project(out, run, i, cols):
             for g in range(PASSES):
                 nc.tensor.matmul_mx(
                     out=out,
-                    lhsT=x_codes[pair][:, i, g, :].bitcast(FP8X4),
-                    lhsT_scale=x_scales[pair][:, i, g, :],
+                    lhsT=x_codes[run][:, i, g, :].bitcast(FP8X4),
+                    lhsT_scale=x_scales[run][:, i, g, :],
                     rhs=w_codes[:, g, cols].bitcast(FP8X4),
                     rhs_scale=w_scales[:, g, cols],
                     start=(g == 0),
                     stop=(g == PASSES - 1),
                 )
 
-        def multiply_and_rotate(pair):
-            first = pair * PAIR
-            place = first % STORE_TILES
+        qk_sb = {}
+        v_sb = {}
+        qk_ps = {}
+
+        def multiply(run):
+            group = run * RUN_TILES // STORE_TILES
+            place = run * RUN_TILES % STORE_TILES
             if place == 0:
-                results["qk"] = result_pool.tile([P, 2, STORE_TILES, FEATURES], F32, name="qk_sb")
-                results["v"] = result_pool.tile([P, STORE_TILES, FEATURES], F32, name="v_sb")
-            qk_sb = results["qk"]
-            v_sb = results["v"]
+                qk_sb[group] = result_pool.tile([P, 2, STORE_TILES, FEATURES], F32, name="qk_sb")
+                v_sb[group] = result_pool.tile([P, STORE_TILES, FEATURES], F32, name="v_sb")
+            v_ps = v_pool.tile([P, RUN_TILES, FEATURES], F32, name="v_ps")
+            for a in range(RUN_PAIRS):
+                if run >= RUNS - TAIL_RUNS:
+                    qk_ps[a] = xt_pool.tile([P, PAIR, 2 * FEATURES], F32, name="xt")
+                else:
+                    qk_ps[a] = qk_pool.tile([P, PAIR, 2 * FEATURES], F32, name="qk_ps")
+                for i in range(PAIR):
+                    project(qk_ps[a][:, i, :], run, a * PAIR + i, slice(0, 2 * FEATURES))
+                    project(v_ps[:, a * PAIR + i, :], run, a * PAIR + i, slice(2 * FEATURES, 3 * FEATURES))
+            nc.scalar.copy(out=v_sb[group][:, place : place + RUN_TILES, :], in_=v_ps[:])
 
-            qk_ps = qk_pool.tile([P, PAIR, 2 * FEATURES], F32, name="qk_ps")
-            v_ps = v_pool.tile([P, PAIR, FEATURES], F32, name="v_ps")
-            for i in range(PAIR):
-                project(qk_ps[:, i, :], pair, i, slice(0, 2 * FEATURES))
-                project(v_ps[:, i, :], pair, i, slice(2 * FEATURES, 3 * FEATURES))
+        prods = {}
 
-            nc.scalar.copy(out=v_sb[:, place : place + PAIR, :], in_=v_ps[:])
-
-            table_shape = [P, PAIR, 2 * HEADS, HEAD_DIM]
-            tiles = slice(first, first + PAIR)
-            cross = cross_pool.tile([P, 2, PAIR, FEATURES], F32, name="cross")
+        def product(run, a, half):
+            first = run * RUN_TILES + a * PAIR
+            table = (table_lo, table_hi)[half]
             nc.vector.tensor_tensor(
-                out=qk_sb[:, :, place : place + PAIR, :].rearrange("p w i f -> p i w f"),
-                in0=qk_ps[:],
-                in1=cos_sb[:, tiles, :].unsqueeze(2).to_broadcast(table_shape),
+                out=prods[half][:, :, a * PAIR : (a + 1) * PAIR, :].rearrange("p w i f -> p i w f"),
+                in0=qk_ps[a][:],
+                in1=table[:, first : first + PAIR, :].unsqueeze(2).to_broadcast([P, PAIR, 2 * HEADS, HEAD_DIM]),
                 op=ALU.mult,
             )
-            nc.vector.tensor_tensor(
-                out=cross[:].rearrange("p w i f -> p i w f"),
-                in0=qk_ps[:],
-                in1=sin_swapped[:, tiles, :].unsqueeze(2).to_broadcast(table_shape),
-                op=ALU.mult,
-            )
+
+        def join(engine, run, at, tiles, half):
+            group = run * RUN_TILES // STORE_TILES
+            place = run * RUN_TILES % STORE_TILES + at
             halves = "p w i (h f j) -> p w (i h) f j"
-            straight_halves = qk_sb[:, :, place : place + PAIR, :].rearrange(halves, f=2, j=HALF)
-            cross_halves = cross[:].rearrange(halves, f=2, j=HALF)
-            nc.gpsimd.tensor_tensor(
-                out=straight_halves[:, :, :, 0, :],
-                in0=straight_halves[:, :, :, 0, :],
-                in1=cross_halves[:, :, :, 1, :],
-                op=ALU.subtract,
-            )
-            nc.gpsimd.tensor_tensor(
-                out=straight_halves[:, :, :, 1, :],
-                in0=straight_halves[:, :, :, 1, :],
-                in1=cross_halves[:, :, :, 0, :],
-                op=ALU.add,
-            )
+            terms = prods[half][:, :, at : at + tiles, :].rearrange(halves, f=2, j=HALF)
+            sums = qk_sb[group][:, :, place : place + tiles, :].rearrange(halves, f=2, j=HALF)
+            engine.tensor_tensor(out=sums[:, :, :, half, :], in0=terms[:, :, :, 0, :], in1=terms[:, :, :, 1, :], op=ALU.add)
 
-            if place + PAIR == STORE_TILES:
-                stored = slice(first + PAIR - STORE_TILES, first + PAIR)
-                nc.sync.dma_start(out=v_rows[:, stored, :], in_=v_sb[:])
-                nc.sync.dma_start(out=q_rows[:, stored, :], in_=qk_sb[:, 0, :, :])
-                nc.sync.dma_start(out=k_rows[:, stored, :], in_=qk_sb[:, 1, :, :])
+        def store_v(first, tiles):
+            group = first // STORE_TILES
+            place = first % STORE_TILES
+            nc.sync.dma_start(out=v_rows[:, first : first + tiles, :], in_=v_sb[group][:, place : place + tiles, :])
 
-        def pairs_of(run):
-            return range(run * RUN_PAIRS, (run + 1) * RUN_PAIRS)
+        def store_qk(first, tiles):
+            group = first // STORE_TILES
+            place = first % STORE_TILES
+            nc.sync.dma_start(out=q_rows[:, first : first + tiles, :], in_=qk_sb[group][:, 0, place : place + tiles, :])
+            nc.sync.dma_start(out=k_rows[:, first : first + tiles, :], in_=qk_sb[group][:, 1, place : place + tiles, :])
 
-        for pair in pairs_of(0):
-            transpose_and_quantise(pair)
-
-        sin_swapped = const.tile([P, ROW_TILES, HEAD_DIM], BF16, name="sin_swapped")
-        nc.vector.tensor_copy(out=sin_swapped[:, :, 0:HALF], in_=sin_sb[:, :, HALF:HEAD_DIM])
-        nc.vector.tensor_copy(out=sin_swapped[:, :, HALF:HEAD_DIM], in_=sin_sb[:, :, 0:HALF])
+        for run in range(LEAD):
+            transpose(run)
+            quantise(run)
 
         for run in range(RUNS):
-            if run + 1 < RUNS:
-                for pair in pairs_of(run + 1):
-                    transpose_and_quantise(pair)
+            if run + LEAD < RUNS:
+                transpose(run + LEAD)
             if run + LOADS_AHEAD < RUNS:
-                load_x(run + LOADS_AHEAD)
-            for pair in pairs_of(run):
-                multiply_and_rotate(pair)
+                load_x(nc.sync, run + LOADS_AHEAD, (RUN_TILES,))
+            multiply(run)
+            if run == 0:
+                make_tables(slice(0, FIRST_TABLE_TILES))
+            if run * RUN_TILES == FIRST_TABLE_TILES:
+                make_tables(slice(FIRST_TABLE_TILES, ROW_TILES))
+            prods[0] = prod_pool.tile([P, 2, RUN_TILES, FEATURES], F32, name="prod_lo")
+            prods[1] = prod_pool.tile([P, 2, RUN_TILES, FEATURES], F32, name="prod_hi")
+            first = run * RUN_TILES
+            if run < RUNS - TAIL_RUNS:
+                for half in range(2):
+                    for a in range(RUN_PAIRS):
+                        product(run, a, half)
+                quantise(run + LEAD)
+                for half in range(2):
+                    join(nc.gpsimd, run, 0, RUN_TILES, half)
+                if (first + RUN_TILES) % STORE_TILES == 0:
+                    store_v(first + RUN_TILES - STORE_TILES, STORE_TILES)
+                    store_qk(first + RUN_TILES - STORE_TILES, STORE_TILES)
+            else:
+                store_v(first, RUN_TILES)
+                for a in range(RUN_PAIRS):
+                    for half in range(2):
+                        product(run, a, half)
+                last = run == RUNS - 1
+                for a in range(RUN_PAIRS):
+                    engine = nc.vector if (last and a == RUN_PAIRS - 1) else nc.gpsimd
+                    for half in range(2):
+                        join(engine, run, a * PAIR, PAIR, half)
+                    store_qk(first + a * PAIR, PAIR)

@@ -30,6 +30,8 @@ LEAD = 2
 LOADS_AHEAD = 6
 STORE_TILES = 8
 FIRST_TABLE_TILES = 8
+SORTED_TILES = (0,)
+FIRST_SORTED_RUN = 4
 TAIL_RUNS = 2
 
 FLOPS = 2 * ROWS * K * 3 * FEATURES
@@ -62,6 +64,7 @@ def tile_groupedqueryattention_pa_t_kernel(
     with ExitStack() as ctx:
         const = ctx.enter_context(tc.tile_pool(name="const", bufs=1))
         x_pool = ctx.enter_context(tc.tile_pool(name="x", bufs=LOADS_AHEAD + 1))
+        sort_pool = ctx.enter_context(tc.tile_pool(name="sorted", bufs=3))
         grouped_pool = ctx.enter_context(tc.tile_pool(name="grouped", bufs=3))
         codes_pool = ctx.enter_context(tc.tile_pool(name="codes", bufs=LEAD + 2))
         prod_pool = ctx.enter_context(tc.tile_pool(name="prod", bufs=3))
@@ -137,6 +140,16 @@ def tile_groupedqueryattention_pa_t_kernel(
         x_codes = {}
         x_scales = {}
 
+        sorted_words = {}
+
+        def sort_words(run):
+            for i in SORTED_TILES:
+                sorted_words[(run, i)] = sort_pool.tile([P, PASSES, 2, P], F32, name="sorted")
+                nc.scalar.copy(
+                    out=sorted_words[(run, i)][:],
+                    in_=x_sb[run][:, i, :].bitcast(F32).rearrange("p (g c u) -> p g u c", g=PASSES, u=2),
+                )
+
         def transpose(run):
             grouped[run] = grouped_pool.tile([P, RUN_TILES, PASSES, P, 4], BF16, name="grouped", align_bytes=64)
             for i in range(RUN_TILES):
@@ -144,11 +157,11 @@ def tile_groupedqueryattention_pa_t_kernel(
                 xt = xt_pool.tile([P, PASSES, 2, P], F32, name="xt")
                 for g in range(PASSES):
                     for u in range(2):
-                        nc.tensor.transpose(
-                            xt[:, g, u, :],
-                            words[:, g * WORDS_PASS + u : (g + 1) * WORDS_PASS : 2],
-                            identity[:],
-                        )
+                        if (run, i) in sorted_words:
+                            every_second = sorted_words[(run, i)][:, g, u, :]
+                        else:
+                            every_second = words[:, g * WORDS_PASS + u : (g + 1) * WORDS_PASS : 2]
+                        nc.tensor.transpose(xt[:, g, u, :], every_second, identity[:])
                 nc.scalar.copy(
                     out=grouped[run][:, i, :, :, :]
                     .rearrange("p g r j -> p (g r j)")
@@ -237,6 +250,8 @@ def tile_groupedqueryattention_pa_t_kernel(
         for run in range(RUNS):
             if run + LEAD < RUNS:
                 transpose(run + LEAD)
+            if FIRST_SORTED_RUN <= run + LEAD + 1 < RUNS:
+                sort_words(run + LEAD + 1)
             if run + LOADS_AHEAD < RUNS:
                 load_x(nc.sync, run + LOADS_AHEAD, (RUN_TILES,))
             multiply(run)

@@ -30,7 +30,7 @@ LEAD = 2
 LOADS_AHEAD = 6
 STORE_TILES = 8
 FIRST_TABLE_TILES = 8
-SORTED_TILES = (0,)
+SORTED_TILES = (3,)
 FIRST_SORTED_RUN = 4
 TAIL_RUNS = 2
 

@@ -110,11 +110,11 @@ def tile_groupedqueryattention_pa_t_kernel(
                 )
 
         load_x(nc.scalar, 0, (1, 1, 2))
-        load_scales(range(0, 5))
-        load_x(nc.sync, 1, (4,))
-        load_scales(range(5, 9))
-        load_x(nc.sync, 2, (4,))
-        load_scales(range(9, 12))
+        load_scales(range(0, 4))
+        load_x(nc.sync, 1, (2, 2))
+        load_scales(range(4, 8))
+        load_x(nc.sync, 2, (2, 2))
+        load_scales(range(8, 12))
         for w, (words, scales) in enumerate(weights):
             cols = slice(w * FEATURES, (w + 1) * FEATURES)
             nc.sync.dma_start(

@@ -127,14 +127,16 @@ def tile_groupedqueryattention_pa_t_kernel(
         load_tables(slice(FIRST_TABLE_TILES, ROW_TILES))
         load_x(nc.sync, 5, (4,))
 
-        table_lo = const.tile([P, ROW_TILES, HEAD_DIM], BF16, name="table_lo")
-        table_hi = const.tile([P, ROW_TILES, HEAD_DIM], BF16, name="table_hi")
+        tables = const.tile([P, ROW_TILES // PAIR, 2, PAIR, HEAD_DIM], BF16, name="tables")
 
         def make_tables(tiles):
-            nc.vector.tensor_copy(out=table_lo[:, tiles, 0:HALF], in_=cos_sb[:, tiles, 0:HALF])
-            nc.vector.tensor_scalar_mul(out=table_lo[:, tiles, HALF:HEAD_DIM], in0=sin_sb[:, tiles, 0:HALF], scalar1=-1.0)
-            nc.vector.tensor_copy(out=table_hi[:, tiles, 0:HALF], in_=sin_sb[:, tiles, HALF:HEAD_DIM])
-            nc.vector.tensor_copy(out=table_hi[:, tiles, HALF:HEAD_DIM], in_=cos_sb[:, tiles, HALF:HEAD_DIM])
+            pairs = slice(tiles.start // PAIR, tiles.stop // PAIR)
+            cos = cos_sb[:, tiles, :].rearrange("p (n i) d -> p n i d", i=PAIR)
+            sin = sin_sb[:, tiles, :].rearrange("p (n i) d -> p n i d", i=PAIR)
+            nc.vector.tensor_copy(out=tables[:, pairs, 0, :, 0:HALF], in_=cos[:, :, :, 0:HALF])
+            nc.vector.tensor_scalar_mul(out=tables[:, pairs, 0, :, HALF:HEAD_DIM], in0=sin[:, :, :, 0:HALF], scalar1=-1.0)
+            nc.vector.tensor_copy(out=tables[:, pairs, 1, :, 0:HALF], in_=sin[:, :, :, HALF:HEAD_DIM])
+            nc.vector.tensor_copy(out=tables[:, pairs, 1, :, HALF:HEAD_DIM], in_=cos[:, :, :, HALF:HEAD_DIM])
 
         grouped = {}
         x_codes = {}
@@ -214,23 +216,24 @@ def tile_groupedqueryattention_pa_t_kernel(
 
         prods = {}
 
-        def product(run, a, half):
-            first = run * RUN_TILES + a * PAIR
-            table = (table_lo, table_hi)[half]
+        def product(run, a):
+            pair = run * RUN_PAIRS + a
             nc.vector.tensor_tensor(
-                out=prods[half][:, :, a * PAIR : (a + 1) * PAIR, :].rearrange("p w i f -> p i w f"),
-                in0=qk_ps[a][:],
-                in1=table[:, first : first + PAIR, :].unsqueeze(2).to_broadcast([P, PAIR, 2 * HEADS, HEAD_DIM]),
+                out=prods[run][:, :, a * PAIR : (a + 1) * PAIR, :].rearrange("p e i c -> p e (i c)"),
+                in0=qk_ps[a][:].rearrange("p i c -> p (i c)").unsqueeze(1).to_broadcast([P, 2, PAIR * 2 * FEATURES]),
+                in1=tables[:, pair, :, :, :]
+                .rearrange("p e i d -> p (e i) d")
+                .unsqueeze(2)
+                .to_broadcast([P, 2 * PAIR, 2 * HEADS, HEAD_DIM]),
                 op=ALU.mult,
             )
 
-        def join(engine, run, at, tiles, half):
+        def join(engine, run, at, tiles):
             group = run * RUN_TILES // STORE_TILES
             place = run * RUN_TILES % STORE_TILES + at
-            halves = "p w i (h f j) -> p w (i h) f j"
-            terms = prods[half][:, :, at : at + tiles, :].rearrange(halves, f=2, j=HALF)
-            sums = qk_sb[group][:, :, place : place + tiles, :].rearrange(halves, f=2, j=HALF)
-            engine.tensor_tensor(out=sums[:, :, :, half, :], in0=terms[:, :, :, 0, :], in1=terms[:, :, :, 1, :], op=ALU.add)
+            terms = prods[run][:, :, at : at + tiles, :].rearrange("p e i (c f j) -> p (i c) e f j", f=2, j=HALF)
+            sums = qk_sb[group][:, :, place : place + tiles, :].rearrange("p w i f -> p i w f")
+            engine.tensor_tensor(out=sums, in0=terms[:, :, :, 0, :], in1=terms[:, :, :, 1, :], op=ALU.add)
 
         def store_v(first, tiles):
             group = first // STORE_TILES
@@ -259,27 +262,22 @@ def tile_groupedqueryattention_pa_t_kernel(
                 make_tables(slice(0, FIRST_TABLE_TILES))
             if run * RUN_TILES == FIRST_TABLE_TILES:
                 make_tables(slice(FIRST_TABLE_TILES, ROW_TILES))
-            prods[0] = prod_pool.tile([P, 2, RUN_TILES, FEATURES], F32, name="prod_lo")
-            prods[1] = prod_pool.tile([P, 2, RUN_TILES, FEATURES], F32, name="prod_hi")
+            prods[run] = prod_pool.tile([P, 2, RUN_TILES, 2 * FEATURES], F32, name="prod")
             first = run * RUN_TILES
             if run < RUNS - TAIL_RUNS:
-                for half in range(2):
-                    for a in range(RUN_PAIRS):
-                        product(run, a, half)
+                for a in range(RUN_PAIRS):
+                    product(run, a)
                 quantise(run + LEAD)
-                for half in range(2):
-                    join(nc.gpsimd, run, 0, RUN_TILES, half)
+                join(nc.gpsimd, run, 0, RUN_TILES)
                 if (first + RUN_TILES) % STORE_TILES == 0:
                     store_v(first + RUN_TILES - STORE_TILES, STORE_TILES)
                     store_qk(first + RUN_TILES - STORE_TILES, STORE_TILES)
             else:
                 store_v(first, RUN_TILES)
                 for a in range(RUN_PAIRS):
-                    for half in range(2):
-                        product(run, a, half)
+                    product(run, a)
                 last = run == RUNS - 1
                 for a in range(RUN_PAIRS):
                     engine = nc.vector if (last and a == RUN_PAIRS - 1) else nc.gpsimd
-                    for half in range(2):
-                        join(engine, run, a * PAIR, PAIR, half)
+                    join(engine, run, a * PAIR, PAIR)
                     store_qk(first + a * PAIR, PAIR)

@@ -27,7 +27,7 @@ RUN_PAIRS = 2
 RUN_TILES = RUN_PAIRS * PAIR
 RUNS = ROW_TILES // RUN_TILES
 LEAD = 2
-LOADS_AHEAD = 6
+LOADS_AHEAD = 11
 STORE_TILES = 8
 FIRST_TABLE_TILES = 8
 SORTED_TILES = (3,)
@@ -125,7 +125,8 @@ def tile_groupedqueryattention_pa_t_kernel(
         load_x(nc.sync, 3, (4,))
         load_x(nc.sync, 4, (4,))
         load_tables(slice(FIRST_TABLE_TILES, ROW_TILES))
-        load_x(nc.sync, 5, (4,))
+        for run in range(5, LOADS_AHEAD):
+            load_x(nc.sync, run, (RUN_TILES,))
 
         tables = const.tile([P, ROW_TILES // PAIR, 2, PAIR, HEAD_DIM], BF16, name="tables")
 

@@ -70,8 +70,8 @@ def tile_groupedqueryattention_pa_t_kernel(
         prod_pool = ctx.enter_context(tc.tile_pool(name="prod", bufs=3))
         result_pool = ctx.enter_context(tc.tile_pool(name="result", bufs=3))
         xt_pool = ctx.enter_context(tc.psum_pool(name="xt", bufs=RUN_TILES))
-        qk_pool = ctx.enter_context(tc.psum_pool(name="qk", bufs=RUN_PAIRS))
-        v_pool = ctx.enter_context(tc.psum_pool(name="v", bufs=2))
+        qk_pool = ctx.enter_context(tc.psum_pool(name="qk", bufs=3))
+        v_pool = ctx.enter_context(tc.psum_pool(name="v", bufs=1))
         ctx.enter_context(tc.manual_schedule())
 
         identity = const.tile([P, P], F32, name="identity")

@@ -26,11 +26,12 @@ PAIR = 2
 RUN_PAIRS = 2
 RUN_TILES = RUN_PAIRS * PAIR
 RUNS = ROW_TILES // RUN_TILES
+UNITS = RUN_TILES * PASSES
 LEAD = 2
 LOADS_AHEAD = 11
 STORE_TILES = 8
 FIRST_TABLE_TILES = 8
-SORTED_TILES = (3,)
+SORTED_UNITS = 3
 FIRST_SORTED_RUN = 4
 TAIL_RUNS = 2
 
@@ -146,12 +147,12 @@ def tile_groupedqueryattention_pa_t_kernel(
         sorted_words = {}
 
         def sort_words(run):
-            for i in SORTED_TILES:
-                sorted_words[(run, i)] = sort_pool.tile([P, PASSES, 2, P], F32, name="sorted")
-                nc.scalar.copy(
-                    out=sorted_words[(run, i)][:],
-                    in_=x_sb[run][:, i, :].bitcast(F32).rearrange("p (g c u) -> p g u c", g=PASSES, u=2),
-                )
+            sorted_words[run] = sort_pool.tile([P, SORTED_UNITS, 2, P], F32, name="sorted")
+            words = x_sb[run][:].rearrange("p i k -> p (i k)").bitcast(F32)
+            nc.scalar.copy(
+                out=sorted_words[run][:],
+                in_=words[:, (UNITS - SORTED_UNITS) * WORDS_PASS :].rearrange("p (n c u) -> p n u c", u=2, c=P),
+            )
 
         def transpose(run):
             grouped[run] = grouped_pool.tile([P, RUN_TILES, PASSES, P, 4], BF16, name="grouped", align_bytes=64)
@@ -160,8 +161,9 @@ def tile_groupedqueryattention_pa_t_kernel(
                 xt = xt_pool.tile([P, PASSES, 2, P], F32, name="xt")
                 for g in range(PASSES):
                     for u in range(2):
-                        if (run, i) in sorted_words:
-                            every_second = sorted_words[(run, i)][:, g, u, :]
+                        unit = i * PASSES + g - (UNITS - SORTED_UNITS)
+                        if run in sorted_words and unit >= 0:
+                            every_second = sorted_words[run][:, unit, u, :]
                         else:
                             every_second = words[:, g * WORDS_PASS + u : (g + 1) * WORDS_PASS : 2]
                         nc.tensor.transpose(xt[:, g, u, :], every_second, identity[:])
@@ -212,7 +214,8 @@ def tile_groupedqueryattention_pa_t_kernel(
                     qk_ps[a] = qk_pool.tile([P, PAIR, 2 * FEATURES], F32, name="qk_ps")
                 for i in range(PAIR):
                     project(qk_ps[a][:, i, :], run, a * PAIR + i, slice(0, 2 * FEATURES))
-                    project(v_ps[:, a * PAIR + i, :], run, a * PAIR + i, slice(2 * FEATURES, 3 * FEATURES))
+            for i in range(RUN_TILES):
+                project(v_ps[:, i, :], run, i, slice(2 * FEATURES, 3 * FEATURES))
             nc.scalar.copy(out=v_sb[group][:, place : place + RUN_TILES, :], in_=v_ps[:])
 
         prods = {}
@@ -252,13 +255,16 @@ def tile_groupedqueryattention_pa_t_kernel(
             quantise(run)
 
         for run in range(RUNS):
-            if run + LEAD < RUNS:
+            last_transposes = run + LEAD == RUNS - 1
+            if run + LEAD < RUNS and not last_transposes:
                 transpose(run + LEAD)
             if FIRST_SORTED_RUN <= run + LEAD + 1 < RUNS:
                 sort_words(run + LEAD + 1)
             if run + LOADS_AHEAD < RUNS:
                 load_x(nc.sync, run + LOADS_AHEAD, (RUN_TILES,))
             multiply(run)
+            if last_transposes:
+                transpose(run + LEAD)
             if run == 0:
                 make_tables(slice(0, FIRST_TABLE_TILES))
             if run * RUN_TILES == FIRST_TABLE_TILES:

@@ -28,11 +28,12 @@ RUN_TILES = RUN_PAIRS * PAIR
 RUNS = ROW_TILES // RUN_TILES
 UNITS = RUN_TILES * PASSES
 LEAD = 2
-LOADS_AHEAD = 11
+LOADS_AHEAD = 8
 STORE_TILES = 8
 FIRST_TABLE_TILES = 8
 SORTED_UNITS = 3
-FIRST_SORTED_RUN = 4
+FIRST_SORTED_RUN = 5
+PASSES_FIRST = (1, RUNS - 1 - LEAD)
 TAIL_RUNS = 2
 
 FLOPS = 2 * ROWS * K * 3 * FEATURES
@@ -69,7 +70,7 @@ def tile_groupedqueryattention_pa_t_kernel(
         grouped_pool = ctx.enter_context(tc.tile_pool(name="grouped", bufs=3))
         codes_pool = ctx.enter_context(tc.tile_pool(name="codes", bufs=LEAD + 2))
         prod_pool = ctx.enter_context(tc.tile_pool(name="prod", bufs=3))
-        result_pool = ctx.enter_context(tc.tile_pool(name="result", bufs=3))
+        result_pool = ctx.enter_context(tc.tile_pool(name="result", bufs=4))
         xt_pool = ctx.enter_context(tc.psum_pool(name="xt", bufs=RUN_TILES))
         qk_pool = ctx.enter_context(tc.psum_pool(name="qk", bufs=3))
         v_pool = ctx.enter_context(tc.psum_pool(name="v", bufs=1))
@@ -175,14 +176,16 @@ def tile_groupedqueryattention_pa_t_kernel(
                     in_=xt[:].rearrange("p g u r -> p g r u"),
                 )
 
-        def quantise(run):
+        def quantise(run, parts=1):
             x_codes[run] = codes_pool.tile([P, RUN_TILES, PASSES, P], U32, name="x_codes", align_bytes=64)
             x_scales[run] = codes_pool.tile([P, RUN_TILES, PASSES, P], U8, name="x_scales", align_bytes=64)
-            nc.vector.quantize_mx(
-                out=x_codes[run][:].rearrange("p i g r -> p (i g r)").bitcast(FP8X4),
-                scales=x_scales[run][:].rearrange("p i g r -> p (i g r)"),
-                in_=grouped[run][:].rearrange("p i g r j -> p (i g r j)"),
-            )
+            tiles = RUN_TILES // parts
+            for at in range(0, RUN_TILES, tiles):
+                nc.vector.quantize_mx(
+                    out=x_codes[run][:, at : at + tiles, :, :].rearrange("p i g r -> p (i g r)").bitcast(FP8X4),
+                    scales=x_scales[run][:, at : at + tiles, :, :].rearrange("p i g r -> p (i g r)"),
+                    in_=grouped[run][:, at : at + tiles, :, :, :].rearrange("p i g r j -> p (i g r j)"),
+                )
 
         def project(out, run, i, cols):
             for g in range(PASSES):
@@ -206,7 +209,12 @@ def tile_groupedqueryattention_pa_t_kernel(
             if place == 0:
                 qk_sb[group] = result_pool.tile([P, 2, STORE_TILES, FEATURES], F32, name="qk_sb")
                 v_sb[group] = result_pool.tile([P, STORE_TILES, FEATURES], F32, name="v_sb")
-            v_ps = v_pool.tile([P, RUN_TILES, FEATURES], F32, name="v_ps")
+            if run in PASSES_FIRST:
+                v_ps = xt_pool.tile([P, RUN_TILES, FEATURES], F32, name="xt")
+            elif run == RUNS - 1:
+                v_ps = qk_pool.tile([P, RUN_TILES, FEATURES], F32, name="qk_ps")
+            else:
+                v_ps = v_pool.tile([P, RUN_TILES, FEATURES], F32, name="v_ps")
             for a in range(RUN_PAIRS):
                 if run >= RUNS - TAIL_RUNS:
                     qk_ps[a] = xt_pool.tile([P, PAIR, 2 * FEATURES], F32, name="xt")
@@ -214,8 +222,7 @@ def tile_groupedqueryattention_pa_t_kernel(
                     qk_ps[a] = qk_pool.tile([P, PAIR, 2 * FEATURES], F32, name="qk_ps")
                 for i in range(PAIR):
                     project(qk_ps[a][:, i, :], run, a * PAIR + i, slice(0, 2 * FEATURES))
-            for i in range(RUN_TILES):
-                project(v_ps[:, i, :], run, i, slice(2 * FEATURES, 3 * FEATURES))
+                    project(v_ps[:, a * PAIR + i, :], run, a * PAIR + i, slice(2 * FEATURES, 3 * FEATURES))
             nc.scalar.copy(out=v_sb[group][:, place : place + RUN_TILES, :], in_=v_ps[:])
 
         prods = {}
@@ -255,15 +262,15 @@ def tile_groupedqueryattention_pa_t_kernel(
             quantise(run)
 
         for run in range(RUNS):
-            last_transposes = run + LEAD == RUNS - 1
-            if run + LEAD < RUNS and not last_transposes:
+            passes_first = run in PASSES_FIRST
+            if run + LEAD < RUNS and not passes_first:
                 transpose(run + LEAD)
             if FIRST_SORTED_RUN <= run + LEAD + 1 < RUNS:
                 sort_words(run + LEAD + 1)
             if run + LOADS_AHEAD < RUNS:
                 load_x(nc.sync, run + LOADS_AHEAD, (RUN_TILES,))
             multiply(run)
-            if last_transposes:
+            if passes_first:
                 transpose(run + LEAD)
             if run == 0:
                 make_tables(slice(0, FIRST_TABLE_TILES))
@@ -274,7 +281,7 @@ def tile_groupedqueryattention_pa_t_kernel(
             if run < RUNS - TAIL_RUNS:
                 for a in range(RUN_PAIRS):
                     product(run, a)
-                quantise(run + LEAD)
+                quantise(run + LEAD, parts=2 if run + LEAD == RUNS - 1 else 1)
                 join(nc.gpsimd, run, 0, RUN_TILES)
                 if (first + RUN_TILES) % STORE_TILES == 0:
                     store_v(first + RUN_TILES - STORE_TILES, STORE_TILES)

@@ -32,8 +32,9 @@ LOADS_AHEAD = 8
 STORE_TILES = 8
 FIRST_TABLE_TILES = 8
 SORTED_UNITS = 3
-FIRST_SORTED_RUN = 5
-PASSES_FIRST = (1, RUNS - 1 - LEAD)
+FIRST_SORTED_RUN = 6
+PASSES_FIRST = (1,)
+SHORT_STORES = 4
 TAIL_RUNS = 2
 
 FLOPS = 2 * ROWS * K * 3 * FEATURES
@@ -125,8 +126,8 @@ def tile_groupedqueryattention_pa_t_kernel(
             )
         load_tables(slice(0, FIRST_TABLE_TILES))
         load_x(nc.sync, 3, (4,))
-        load_x(nc.sync, 4, (4,))
         load_tables(slice(FIRST_TABLE_TILES, ROW_TILES))
+        load_x(nc.sync, 4, (2, 2))
         for run in range(5, LOADS_AHEAD):
             load_x(nc.sync, run, (RUN_TILES,))
 
@@ -176,16 +177,14 @@ def tile_groupedqueryattention_pa_t_kernel(
                     in_=xt[:].rearrange("p g u r -> p g r u"),
                 )
 
-        def quantise(run, parts=1):
+        def quantise(run):
             x_codes[run] = codes_pool.tile([P, RUN_TILES, PASSES, P], U32, name="x_codes", align_bytes=64)
             x_scales[run] = codes_pool.tile([P, RUN_TILES, PASSES, P], U8, name="x_scales", align_bytes=64)
-            tiles = RUN_TILES // parts
-            for at in range(0, RUN_TILES, tiles):
-                nc.vector.quantize_mx(
-                    out=x_codes[run][:, at : at + tiles, :, :].rearrange("p i g r -> p (i g r)").bitcast(FP8X4),
-                    scales=x_scales[run][:, at : at + tiles, :, :].rearrange("p i g r -> p (i g r)"),
-                    in_=grouped[run][:, at : at + tiles, :, :, :].rearrange("p i g r j -> p (i g r j)"),
-                )
+            nc.vector.quantize_mx(
+                out=x_codes[run][:].rearrange("p i g r -> p (i g r)").bitcast(FP8X4),
+                scales=x_scales[run][:].rearrange("p i g r -> p (i g r)"),
+                in_=grouped[run][:].rearrange("p i g r j -> p (i g r j)"),
+            )
 
         def project(out, run, i, cols):
             for g in range(PASSES):
@@ -211,7 +210,7 @@ def tile_groupedqueryattention_pa_t_kernel(
                 v_sb[group] = result_pool.tile([P, STORE_TILES, FEATURES], F32, name="v_sb")
             if run in PASSES_FIRST:
                 v_ps = xt_pool.tile([P, RUN_TILES, FEATURES], F32, name="xt")
-            elif run == RUNS - 1:
+            elif run >= RUNS - TAIL_RUNS:
                 v_ps = qk_pool.tile([P, RUN_TILES, FEATURES], F32, name="qk_ps")
             else:
                 v_ps = v_pool.tile([P, RUN_TILES, FEATURES], F32, name="v_ps")
@@ -274,24 +273,28 @@ def tile_groupedqueryattention_pa_t_kernel(
                 transpose(run + LEAD)
             if run == 0:
                 make_tables(slice(0, FIRST_TABLE_TILES))
-            if run * RUN_TILES == FIRST_TABLE_TILES:
-                make_tables(slice(FIRST_TABLE_TILES, ROW_TILES))
             prods[run] = prod_pool.tile([P, 2, RUN_TILES, 2 * FEATURES], F32, name="prod")
             first = run * RUN_TILES
+            group = first // STORE_TILES * STORE_TILES
             if run < RUNS - TAIL_RUNS:
                 for a in range(RUN_PAIRS):
                     product(run, a)
-                quantise(run + LEAD, parts=2 if run + LEAD == RUNS - 1 else 1)
-                join(nc.gpsimd, run, 0, RUN_TILES)
-                if (first + RUN_TILES) % STORE_TILES == 0:
-                    store_v(first + RUN_TILES - STORE_TILES, STORE_TILES)
-                    store_qk(first + RUN_TILES - STORE_TILES, STORE_TILES)
+                    if run == 1 and a == 0:
+                        make_tables(slice(FIRST_TABLE_TILES, ROW_TILES))
+                quantise(run + LEAD)
             else:
-                store_v(first, RUN_TILES)
                 for a in range(RUN_PAIRS):
                     product(run, a)
-                last = run == RUNS - 1
+            if run < RUNS - 1:
+                join(nc.gpsimd, run, 0, RUN_TILES)
+            if run >= RUNS - SHORT_STORES:
+                store_v(first, RUN_TILES)
+                if run > RUNS - SHORT_STORES:
+                    store_qk(first - RUN_TILES, RUN_TILES)
+            elif first + RUN_TILES == group + STORE_TILES:
+                store_v(group, STORE_TILES)
+                store_qk(group, STORE_TILES)
+            if run == RUNS - 1:
                 for a in range(RUN_PAIRS):
-                    engine = nc.vector if (last and a == RUN_PAIRS - 1) else nc.gpsimd
-                    join(engine, run, a * PAIR, PAIR)
+                    join(nc.vector, run, a * PAIR, PAIR)
                     store_qk(first + a * PAIR, PAIR)

@@ -32,7 +32,7 @@ LOADS_AHEAD = 8
 STORE_TILES = 8
 FIRST_TABLE_TILES = 8
 SORTED_UNITS = 3
-FIRST_SORTED_RUN = 6
+FIRST_SORTED_RUN = 5
 PASSES_FIRST = (1,)
 SHORT_STORES = 4
 TAIL_RUNS = 2
@@ -112,7 +112,7 @@ def tile_groupedqueryattention_pa_t_kernel(
                     in_=scales[:, 4 * quadrant : 4 * quadrant + 4, :].rearrange("g r n -> r g n").bitcast(I32),
                 )
 
-        load_x(nc.scalar, 0, (1, 1, 2))
+        load_x(nc.sync, 0, (1, 1, 2))
         load_scales(range(0, 4))
         load_x(nc.sync, 1, (2, 2))
         load_scales(range(4, 8))

from contextlib import ExitStack

import concourse.mybir as mybir
from concourse.masks import make_identity

BF16 = mybir.dt.bfloat16
F32 = mybir.dt.float32
I32 = mybir.dt.int32
U32 = mybir.dt.uint32
U8 = mybir.dt.uint8
FP8X4 = mybir.dt.float8_e4m3fn_x4
ALU = mybir.AluOpType

P = 128
ROWS = 8192
K = 1024
K_PASS = 4 * P
PASSES = K // K_PASS
WORDS_PASS = K_PASS // 2
HEADS = 4
HEAD_DIM = 32
HALF = HEAD_DIM // 2
FEATURES = HEADS * HEAD_DIM
ROW_TILES = ROWS // P
PAIR = 2
RUN_PAIRS = 2
RUN_TILES = RUN_PAIRS * PAIR
RUNS = ROW_TILES // RUN_TILES
UNITS = RUN_TILES * PASSES
LEAD = 2
LOADS_AHEAD = 8
STORE_TILES = 8
FIRST_TABLE_TILES = 8
SORTED_UNITS = 3
FIRST_SORTED_RUN = 5
PASSES_FIRST = (1,)
SHORT_STORES = 4
TAIL_RUNS = 2

FLOPS = 2 * ROWS * K * 3 * FEATURES


def tile_groupedqueryattention_pa_t_kernel(
    tc,
    x,
    w_q_words,
    w_q_scales,
    w_k_words,
    w_k_scales,
    w_v_words,
    w_v_scales,
    cos_tab,
    sin_tab,
    out_0,
    out_1,
    out_2,
):
    nc = tc.nc

    x_rows = x.rearrange("(p t) k -> p t k", t=ROW_TILES)
    cos_rows = cos_tab.rearrange("(p t) d -> p t d", t=ROW_TILES)
    sin_rows = sin_tab.rearrange("(p t) d -> p t d", t=ROW_TILES)
    q_rows = out_0.rearrange("(p t) h d -> p t (h d)", t=ROW_TILES)
    k_rows = out_1.rearrange("(p t) h d -> p t (h d)", t=ROW_TILES)
    v_rows = out_2.rearrange("(p t) h d -> p t (h d)", t=ROW_TILES)

    with ExitStack() as ctx:
        const = ctx.enter_context(tc.tile_pool(name="const", bufs=1))
        x_pool = ctx.enter_context(tc.tile_pool(name="x", bufs=LOADS_AHEAD + 1))
        sort_pool = ctx.enter_context(tc.tile_pool(name="sorted", bufs=3))
        grouped_pool = ctx.enter_context(tc.tile_pool(name="grouped", bufs=3))
        codes_pool = ctx.enter_context(tc.tile_pool(name="codes", bufs=LEAD + 2))
        prod_pool = ctx.enter_context(tc.tile_pool(name="prod", bufs=3))
        result_pool = ctx.enter_context(tc.tile_pool(name="result", bufs=4))
        xt_pool = ctx.enter_context(tc.psum_pool(name="xt", bufs=RUN_TILES))
        qk_pool = ctx.enter_context(tc.psum_pool(name="qk", bufs=3))
        v_pool = ctx.enter_context(tc.psum_pool(name="v", bufs=1))
        ctx.enter_context(tc.manual_schedule())

        identity = const.tile([P, P], F32, name="identity")
        make_identity(nc, identity[:])

        w_codes = const.tile([P, PASSES, 3 * FEATURES], U32, name="w_codes", align_bytes=64)
        w_scales = const.tile([P, PASSES, 3 * FEATURES], U8, name="w_scales", align_bytes=64)
        nc.vector.memset(w_scales[:].rearrange("p g n -> p (g n)").bitcast(I32), 0)

        x_sb = {}

        def load_x(queue, run, pieces):
            x_sb[run] = x_pool.tile([P, RUN_TILES, K], BF16, name="x_sb")
            at = 0
            for tiles in pieces:
                first = run * RUN_TILES + at
                queue.dma_start(out=x_sb[run][:, at : at + tiles, :], in_=x_rows[:, first : first + tiles, :])
                at += tiles

        weights = ((w_q_words, w_q_scales), (w_k_words, w_k_scales), (w_v_words, w_v_scales))
        cos_sb = const.tile([P, ROW_TILES, HEAD_DIM], BF16, name="cos_sb")
        sin_sb = const.tile([P, ROW_TILES, HEAD_DIM], BF16, name="sin_sb")

        def load_tables(tiles):
            nc.sync.dma_start(out=cos_sb[:, tiles, :], in_=cos_rows[:, tiles, :])
            nc.sync.dma_start(out=sin_sb[:, tiles, :], in_=sin_rows[:, tiles, :])

        def load_scales(which):
            for n in which:
                scales = weights[n // 4][1]
                quadrant = n % 4
                cols = slice((n // 4) * FEATURES, (n // 4 + 1) * FEATURES)
                nc.sync.dma_start(
                    out=w_scales[32 * quadrant : 32 * quadrant + 4, :, cols].bitcast(I32),
                    in_=scales[:, 4 * quadrant : 4 * quadrant + 4, :].rearrange("g r n -> r g n").bitcast(I32),
                )

        load_x(nc.sync, 0, (1, 1, 2))
        load_scales(range(0, 4))
        load_x(nc.sync, 1, (2, 2))
        load_scales(range(4, 8))
        load_x(nc.sync, 2, (2, 2))
        load_scales(range(8, 12))
        for w, (words, scales) in enumerate(weights):
            cols = slice(w * FEATURES, (w + 1) * FEATURES)
            nc.sync.dma_start(
                out=w_codes[:, :, cols].bitcast(I32),
                in_=words.rearrange("g p n t -> p g (n t)").bitcast(I32),
            )
        load_tables(slice(0, FIRST_TABLE_TILES))
        load_x(nc.sync, 3, (4,))
        load_tables(slice(FIRST_TABLE_TILES, ROW_TILES))
        load_x(nc.sync, 4, (2, 2))
        for run in range(5, LOADS_AHEAD):
            load_x(nc.sync, run, (RUN_TILES,))

        tables = const.tile([P, ROW_TILES // PAIR, 2, PAIR, HEAD_DIM], BF16, name="tables")

        def make_tables(tiles):
            pairs = slice(tiles.start // PAIR, tiles.stop // PAIR)
            cos = cos_sb[:, tiles, :].rearrange("p (n i) d -> p n i d", i=PAIR)
            sin = sin_sb[:, tiles, :].rearrange("p (n i) d -> p n i d", i=PAIR)
            nc.vector.tensor_copy(out=tables[:, pairs, 0, :, 0:HALF], in_=cos[:, :, :, 0:HALF])
            nc.vector.tensor_scalar_mul(out=tables[:, pairs, 0, :, HALF:HEAD_DIM], in0=sin[:, :, :, 0:HALF], scalar1=-1.0)
            nc.vector.tensor_copy(out=tables[:, pairs, 1, :, 0:HALF], in_=sin[:, :, :, HALF:HEAD_DIM])
            nc.vector.tensor_copy(out=tables[:, pairs, 1, :, HALF:HEAD_DIM], in_=cos[:, :, :, HALF:HEAD_DIM])

        grouped = {}
        x_codes = {}
        x_scales = {}

        sorted_words = {}

        def sort_words(run):
            sorted_words[run] = sort_pool.tile([P, SORTED_UNITS, 2, P], F32, name="sorted")
            words = x_sb[run][:].rearrange("p i k -> p (i k)").bitcast(F32)
            nc.scalar.copy(
                out=sorted_words[run][:],
                in_=words[:, (UNITS - SORTED_UNITS) * WORDS_PASS :].rearrange("p (n c u) -> p n u c", u=2, c=P),
            )

        def transpose(run):
            grouped[run] = grouped_pool.tile([P, RUN_TILES, PASSES, P, 4], BF16, name="grouped", align_bytes=64)
            for i in range(RUN_TILES):
                words = x_sb[run][:, i, :].bitcast(F32)
                xt = xt_pool.tile([P, PASSES, 2, P], F32, name="xt")
                for g in range(PASSES):
                    for u in range(2):
                        unit = i * PASSES + g - (UNITS - SORTED_UNITS)
                        if run in sorted_words and unit >= 0:
                            every_second = sorted_words[run][:, unit, u, :]
                        else:
                            every_second = words[:, g * WORDS_PASS + u : (g + 1) * WORDS_PASS : 2]
                        nc.tensor.transpose(xt[:, g, u, :], every_second, identity[:])
                nc.scalar.copy(
                    out=grouped[run][:, i, :, :, :]
                    .rearrange("p g r j -> p (g r j)")
                    .bitcast(F32)
                    .rearrange("p (g r u) -> p g r u", g=PASSES, u=2),
                    in_=xt[:].rearrange("p g u r -> p g r u"),
                )

        def quantise(run):
            x_codes[run] = codes_pool.tile([P, RUN_TILES, PASSES, P], U32, name="x_codes", align_bytes=64)
            x_scales[run] = codes_pool.tile([P, RUN_TILES, PASSES, P], U8, name="x_scales", align_bytes=64)
            nc.vector.quantize_mx(
                out=x_codes[run][:].rearrange("p i g r -> p (i g r)").bitcast(FP8X4),
                scales=x_scales[run][:].rearrange("p i g r -> p (i g r)"),
                in_=grouped[run][:].rearrange("p i g r j -> p (i g r j)"),
            )

        def project(out, run, i, cols):
            for g in range(PASSES):
                nc.tensor.matmul_mx(
                    out=out,
                    lhsT=x_codes[run][:, i, g, :].bitcast(FP8X4),
                    lhsT_scale=x_scales[run][:, i, g, :],
                    rhs=w_codes[:, g, cols].bitcast(FP8X4),
                    rhs_scale=w_scales[:, g, cols],
                    start=(g == 0),
                    stop=(g == PASSES - 1),
                )

        qk_sb = {}
        v_sb = {}
        qk_ps = {}

        def multiply(run):
            group = run * RUN_TILES // STORE_TILES
            place = run * RUN_TILES % STORE_TILES
            if place == 0:
                qk_sb[group] = result_pool.tile([P, 2, STORE_TILES, FEATURES], F32, name="qk_sb")
                v_sb[group] = result_pool.tile([P, STORE_TILES, FEATURES], F32, name="v_sb")
            if run in PASSES_FIRST:
                v_ps = xt_pool.tile([P, RUN_TILES, FEATURES], F32, name="xt")
            elif run >= RUNS - TAIL_RUNS:
                v_ps = qk_pool.tile([P, RUN_TILES, FEATURES], F32, name="qk_ps")
            else:
                v_ps = v_pool.tile([P, RUN_TILES, FEATURES], F32, name="v_ps")
            for a in range(RUN_PAIRS):
                if run >= RUNS - TAIL_RUNS:
                    qk_ps[a] = xt_pool.tile([P, PAIR, 2 * FEATURES], F32, name="xt")
                else:
                    qk_ps[a] = qk_pool.tile([P, PAIR, 2 * FEATURES], F32, name="qk_ps")
                for i in range(PAIR):
                    project(qk_ps[a][:, i, :], run, a * PAIR + i, slice(0, 2 * FEATURES))
                    project(v_ps[:, a * PAIR + i, :], run, a * PAIR + i, slice(2 * FEATURES, 3 * FEATURES))
            nc.scalar.copy(out=v_sb[group][:, place : place + RUN_TILES, :], in_=v_ps[:])

        prods = {}

        def product(run, a):
            pair = run * RUN_PAIRS + a
            nc.vector.tensor_tensor(
                out=prods[run][:, :, a * PAIR : (a + 1) * PAIR, :].rearrange("p e i c -> p e (i c)"),
                in0=qk_ps[a][:].rearrange("p i c -> p (i c)").unsqueeze(1).to_broadcast([P, 2, PAIR * 2 * FEATURES]),
                in1=tables[:, pair, :, :, :]
                .rearrange("p e i d -> p (e i) d")
                .unsqueeze(2)
                .to_broadcast([P, 2 * PAIR, 2 * HEADS, HEAD_DIM]),
                op=ALU.mult,
            )

        def join(engine, run, at, tiles):
            group = run * RUN_TILES // STORE_TILES
            place = run * RUN_TILES % STORE_TILES + at
            terms = prods[run][:, :, at : at + tiles, :].rearrange("p e i (c f j) -> p (i c) e f j", f=2, j=HALF)
            sums = qk_sb[group][:, :, place : place + tiles, :].rearrange("p w i f -> p i w f")
            engine.tensor_tensor(out=sums, in0=terms[:, :, :, 0, :], in1=terms[:, :, :, 1, :], op=ALU.add)

        def store_v(first, tiles):
            group = first // STORE_TILES
            place = first % STORE_TILES
            nc.sync.dma_start(out=v_rows[:, first : first + tiles, :], in_=v_sb[group][:, place : place + tiles, :])

        def store_qk(first, tiles):
            group = first // STORE_TILES
            place = first % STORE_TILES
            nc.sync.dma_start(out=q_rows[:, first : first + tiles, :], in_=qk_sb[group][:, 0, place : place + tiles, :])
            nc.sync.dma_start(out=k_rows[:, first : first + tiles, :], in_=qk_sb[group][:, 1, place : place + tiles, :])

        for run in range(LEAD):
            transpose(run)
            quantise(run)

        for run in range(RUNS):
            passes_first = run in PASSES_FIRST
            if run + LEAD < RUNS and not passes_first:
                transpose(run + LEAD)
            if FIRST_SORTED_RUN <= run + LEAD + 1 < RUNS:
                sort_words(run + LEAD + 1)
            if run + LOADS_AHEAD < RUNS:
                load_x(nc.sync, run + LOADS_AHEAD, (RUN_TILES,))
            multiply(run)
            if passes_first:
                transpose(run + LEAD)
            if run == 0:
                make_tables(slice(0, FIRST_TABLE_TILES))
            prods[run] = prod_pool.tile([P, 2, RUN_TILES, 2 * FEATURES], F32, name="prod")
            first = run * RUN_TILES
            group = first // STORE_TILES * STORE_TILES
            if run < RUNS - TAIL_RUNS:
                for a in range(RUN_PAIRS):
                    product(run, a)
                    if run == 1 and a == 0:
                        make_tables(slice(FIRST_TABLE_TILES, ROW_TILES))
                quantise(run + LEAD)
            else:
                for a in range(RUN_PAIRS):
                    product(run, a)
            if run < RUNS - 1:
                join(nc.gpsimd, run, 0, RUN_TILES)
            if run >= RUNS - SHORT_STORES:
                store_v(first, RUN_TILES)
                if run > RUNS - SHORT_STORES:
                    store_qk(first - RUN_TILES, RUN_TILES)
            elif first + RUN_TILES == group + STORE_TILES:
                store_v(group, STORE_TILES)
                store_qk(group, STORE_TILES)
            if run == RUNS - 1:
                for a in range(RUN_PAIRS):
                    join(nc.vector, run, a * PAIR, PAIR)
                    store_qk(first + a * PAIR, PAIR)
